import numpy as np
import ml_dtypes


def mxq(x, axis, fmt="e4m3"):
    dtype, down = {"e4m3": (ml_dtypes.float8_e4m3fn, 7), "e5m2": (ml_dtypes.float8_e5m2, 14)}[fmt]
    v = np.moveaxis(np.asarray(x, np.float32).astype(ml_dtypes.bfloat16).astype(np.float64), axis, -1)
    blocks = v.reshape(v.shape[:-1] + (-1, 32))
    amax = np.abs(blocks).max(-1, keepdims=True)
    byte = np.maximum(np.where(amax > 0, np.frexp(amax)[1] - 1 + 127, 0) - down, 1)
    scale = np.exp2(byte - 127.0)
    codes = (blocks / scale).astype(np.float32).astype(dtype).astype(np.float64)
    return np.moveaxis((codes * scale).reshape(v.shape), -1, axis)


WIDE = False


def mx_kscale(k):
    if not WIDE:
        return np.ones(k)
    levels = np.array([10, -10, 5, -5, 0])
    if k % 512:
        return np.exp2(np.random.permutation(np.resize(levels, k // 32))).repeat(32)
    a = np.empty((k // 512, 16))
    for p in range(k // 512):
        a[p, :8] = np.random.permutation(np.resize(levels, 8))
        for g in range(8):
            far = levels[np.abs(levels - a[p, g]) >= 10]
            a[p, g + 8] = far[np.random.randint(len(far))]
    return np.exp2(a.ravel()).repeat(32)


BF16 = ml_dtypes.bfloat16


def bf(x):
    return np.asarray(x, np.float32).astype(BF16)


def f64(x):
    return np.asarray(x).astype(np.float64)


B, OBS, ACT, U, KSUB = 1024, 383, 128, 1024, 2
DT = 1.0 / KSUB
LN_EPS = 1e-5


def mish(v):
    return v * np.tanh(np.log(1.0 + np.exp(v)))


def layer_norm(v, g, b):
    mu = v.mean(-1, keepdims=True)
    var = np.square(v - mu).mean(-1, keepdims=True)
    return (v - mu) / np.sqrt(var + LN_EPS) * g + b


def draw0():
    s, t = mx_kscale(U), mx_kscale(U)
    return {"h0": bf(np.random.standard_normal((B, U)) * s),
            "z": bf(np.random.standard_normal((B, ACT)) * 0.5),
            "k1": bf(np.random.standard_normal((B, ACT))),
            "W1": bf(np.random.standard_normal((U, U)) / np.sqrt(U) / s[:, None]),
            "b1": bf(np.random.standard_normal(U) * 0.3),
            "ln1_g": bf((1.0 + 0.1 * np.random.standard_normal(U)) * t),
            "ln1_b": bf(0.1 * np.random.standard_normal(U) * t),
            "W2": bf(np.random.standard_normal((U, ACT)) / np.sqrt(U) / t[:, None]),
            "b2": bf(np.random.standard_normal(ACT) * 0.3)}


def core(h0, z, k1, W1, b1, ln1_g, ln1_b, W2, b2):
    h1 = layer_norm(mish((mxq(f64(h0), 1, "e4m3") @ mxq(f64(W1), 0, "e4m3")) + f64(b1)), f64(ln1_g), f64(ln1_b))
    k2 = (mxq(h1, 1, "e4m3") @ mxq(f64(W2), 0, "e4m3")) + f64(b2)
    return f64(z) + (DT / 2.0) * (f64(k1) + k2)


def e4m3fn_bytes(y):
    return np.clip(np.asarray(y, np.float64), -448.0, 448.0).astype(np.float32).astype(ml_dtypes.float8_e4m3fn).view(np.uint8)


def e4m3fn_values(b):
    return np.asarray(b, np.uint8).view(ml_dtypes.float8_e4m3fn).astype(np.float64)


def setup_inputs():
    d = draw0()
    x0 = np.asarray(d['h0']).astype(np.float64)
    s = (np.max(np.abs(x0), axis=(0,), keepdims=True) / 448.0).astype(np.float32)
    out = {}
    for k, v in d.items():
        if k == 'h0':
            out['h0_bytes'] = e4m3fn_bytes(x0 / s.astype(np.float64))
            out['h0_scale'] = s
        else:
            out[k] = v
    return out


def reference(h0_bytes, h0_scale, z, k1, W1, b1, ln1_g, ln1_b, W2, b2):
    return core(e4m3fn_values(h0_bytes) * h0_scale.astype(np.float64), z, k1, W1, b1, ln1_g, ln1_b, W2, b2)

@@ -1,0 +1,320 @@
+from contextlib import ExitStack
+
+import concourse.mybir as mybir
+from concourse.masks import make_identity
+
+F32 = mybir.dt.float32
+BF16 = mybir.dt.bfloat16
+U32 = mybir.dt.uint32
+U8 = mybir.dt.uint8
+FP8 = mybir.dt.float8_e4m3fn
+FP8X4 = mybir.dt.float8_e4m3fn_x4
+ALU = mybir.AluOpType
+ACT = mybir.ActivationFunctionType
+
+P = 128
+B = 1024
+U = 1024
+A = 128
+G = 2
+NB = 8
+NT = 8
+EPS = 1e-5
+TINY = 1e-15
+
+FLOPS = 2 * B * U * U + 2 * B * U * A
+
+
+def default_who():
+    who = {}
+    for c in range(2):
+        for g in range(2):
+            who["I", c, g, 0] = "V"
+            who["I", c, g, 1] = "S"
+    for i in range(8):
+        who["HT", i] = "S" if i < 4 else "V"
+        who["NR", i] = "V"
+    for u in range(4):
+        for b in range(4):
+            who["XT", u, b] = "V" if u < 2 else "S"
+    who["SB", 0] = "V"
+    who["SB", 1] = "S"
+    for h in range(2):
+        who["BS", h] = "V" if h == 0 else "S"
+        who["W2", h] = "S"
+    return who
+
+
+def default_order():
+    o = [("SB", 0), ("SB", 1)]
+    o += [("SC", 0), ("I", 0, 0, 0), ("I", 0, 0, 1), ("HT", 0), ("SC", 1), ("I", 0, 1, 0), ("I", 0, 1, 1), ("HT", 1), ("QH", 0), ("SC", 2), ("QW", 0, 0), ("QW", 0, 1), ("HT", 2)]
+    o += [("I", 1, 0, 0), ("I", 1, 0, 1), ("QH", 1), ("SC", 3), ("I", 1, 1, 0), ("I", 1, 1, 1), ("HT", 3), ("QW", 1, 0), ("QH", 2), ("QW", 1, 1)]
+    o += [("B", 0, 0), ("B", 0, 1), ("SG", 0), ("B", 1, 0), ("B", 1, 1), ("SG", 1), ("QH", 3), ("B", 2, 0), ("B", 2, 1), ("SG", 2), ("B", 3, 0), ("B", 3, 1), ("SG", 3)]
+    o += [("LN", i) for i in range(4)]
+    o += [("SC", 4), ("SC", 5), ("HT", 4), ("SC", 6), ("QH", 4), ("HT", 5), ("SC", 7), ("QH", 5), ("HT", 6), ("B", 4, 0), ("B", 4, 1), ("QH", 6), ("HT", 7), ("B", 5, 0), ("QH", 7), ("B", 5, 1)]
+    o += [("TH", 0), ("TH", 1), ("M", 0), ("TH", 2), ("M", 1), ("SG", 4), ("B", 6, 0), ("TH", 3), ("M", 2), ("SQ", 0), ("B", 6, 1), ("SG", 5), ("SQ", 1), ("M", 3), ("SQ", 2), ("B", 7, 0), ("SQ", 3), ("B", 7, 1), ("SG", 6), ("SG", 7)]
+    o += [("NR", 0), ("NR", 1), ("W2", 0), ("W2", 1), ("NR", 2)]
+    o += [("LN", i) for i in range(4, 8)]
+    o += [("XT", 0, b) for b in range(4)] + [("NR", 3), ("IL", 0), ("BS", 0), ("QX", 0)]
+    o += [("XT", 1, b) for b in range(4)] + [("FN", 0), ("IL", 1), ("QX", 1)]
+    o += [("TH", 4), ("TH", 5), ("M", 4), ("TH", 6), ("M", 5), ("SQ", 4), ("TH", 7), ("FN", 1), ("M", 6), ("SQ", 5), ("M", 7), ("SQ", 6), ("BS", 1), ("SQ", 7), ("NR", 4), ("NR", 5), ("NR", 6)]
+    o += [("XT", 2, b) for b in range(4)] + [("NR", 7), ("IL", 2), ("QX", 2)]
+    o += [("XT", 3, b) for b in range(4)] + [("FN", 2), ("IL", 3), ("QX", 3), ("FN", 3)]
+    return o
+
+
+def tile_actorflowode_pb_kernel(tc, h0_bytes, h0_scale, z, k1, W1, b1, ln1_g, ln1_b, W2, b2, out):
+    nc = tc.nc
+    who = default_who()
+    with ExitStack() as ctx:
+        keep = ctx.enter_context(tc.tile_pool(name="keep", bufs=1))
+        work = ctx.enter_context(tc.tile_pool(name="work", bufs=2))
+        psum = ctx.enter_context(tc.psum_pool(name="psum", bufs=2))
+        ctx.enter_context(tc.manual_schedule(engines={mybir.EngineType.Activation, mybir.EngineType.DVE, mybir.EngineType.PE, mybir.EngineType.SP, mybir.EngineType.Pool}))
+
+        h0t = keep.tile([P, NT, U], U8, name="h0t", align_bytes=64)
+        h0v = h0_bytes.rearrange("(p i) k -> p i k", i=NT)
+        sc_raw = keep.tile([P, NB], F32, name="sc_raw")
+        b1_bc = keep.tile([P, U], BF16, name="b1_bc", align_bytes=64)
+        neg_half = keep.tile([P, 1], F32, name="neg_half")
+        warm = keep.tile([P, 1], F32, name="warm")
+        ident = keep.tile([P, P], F32, name="ident")
+        w1v = W1.rearrange("(g p t) (c n) -> c g p t n", p=P, t=4, c=2)
+        w_raw = {}
+        for c in range(2):
+            for g in range(G):
+                w_raw[c, g] = keep.tile([P, 4, 512], BF16, name="w_raw%d%d" % (c, g), align_bytes=64)
+        nc.sync.dma_start(out=sc_raw[:], in_=h0_scale.rearrange("o (p j) -> (o p) j", j=NB))
+        nc.gpsimd.memset(neg_half[:], -0.5)
+        make_identity(nc, ident[:])
+        nc.sync.dma_start(out=h0t[:, 0:2, :], in_=h0v[:, 0:2, :])
+        nc.scalar.activation(out=warm[:], in_=neg_half[:], func=ACT.Sigmoid)
+        nc.sync.dma_start(out=w_raw[0, 0][:], in_=w1v[0, 0])
+        nc.sync.dma_start(out=w_raw[0, 1][:], in_=w1v[0, 1])
+        nc.sync.dma_start(out=h0t[:, 2:4, :], in_=h0v[:, 2:4, :])
+        nc.sync.dma_start(out=w_raw[1, 0][:], in_=w1v[1, 0])
+        nc.sync.dma_start(out=w_raw[1, 1][:], in_=w1v[1, 1])
+        nc.sync.dma_start(out=b1_bc[:], in_=b1.partition_broadcast(P))
+        nc.sync.dma_start(out=h0t[:, 4:8, :], in_=h0v[:, 4:8, :])
+        cols_bf = []
+        for v, vec in enumerate((ln1_g, ln1_b)):
+            col_bf = keep.tile([P, NB], BF16, name="col_bf%d" % v)
+            with nc.allow_non_contiguous_dma(reason="4 neighbouring channels a piece"):
+                nc.sync.dma_start(out=col_bf[:].rearrange("p (g t) -> p g t", t=4), in_=vec.rearrange("(g p t) -> p g t", p=P, t=4))
+            cols_bf.append(col_bf)
+        z_sb = keep.tile([P, NT, A], BF16, name="z_sb", align_bytes=64)
+        k1_sb = keep.tile([P, NT, A], BF16, name="k1_sb", align_bytes=64)
+        b2_bc = keep.tile([P, A], BF16, name="b2_bc", align_bytes=64)
+        nc.sync.dma_start(out=z_sb[:], in_=z.rearrange("(p i) a -> p i a", i=NT))
+        nc.sync.dma_start(out=k1_sb[:], in_=k1.rearrange("(p i) a -> p i a", i=NT))
+        nc.sync.dma_start(out=b2_bc[:], in_=b2.partition_broadcast(P))
+        w2_raw = keep.tile([P, G, 4, A], BF16, name="w2_raw", align_bytes=64)
+        for g in range(G):
+            nc.sync.dma_start(out=w2_raw[:, g], in_=W2.rearrange("(g p t) n -> g p t n", p=P, t=4)[g])
+        out_v = out.rearrange("(p i) a -> p i a", i=NT)
+
+        tiny_col = keep.tile([P, 1], F32, name="tiny_col")
+        nc.gpsimd.tensor_scalar(out=tiny_col[:], in0=neg_half[:], scalar1=-2.0 * TINY, scalar2=0.0, op0=ALU.mult, op1=ALU.add)
+        ident_bf = keep.tile([P, P], BF16, name="ident_bf")
+        quarter_bf = keep.tile([P, P], BF16, name="quarter_bf")
+        ones_bf = keep.tile([P, P], BF16, name="ones_bf")
+        nc.gpsimd.tensor_scalar(out=ident_bf[:], in0=ident[:], scalar1=1.0, scalar2=0.0, op0=ALU.mult, op1=ALU.add)
+        nc.gpsimd.tensor_scalar(out=quarter_bf[:], in0=ident[:], scalar1=0.25, scalar2=0.0, op0=ALU.mult, op1=ALU.add)
+        nc.gpsimd.memset(ones_bf[:], 2.0**-9)
+        cols = keep.tile([P, 2, NB], F32, name="cols")
+        for v in range(2):
+            nc.gpsimd.tensor_scalar(out=cols[:, v, :], in0=cols_bf[v][:], scalar1=1.0, scalar2=0.0, op0=ALU.mult, op1=ALU.add)
+
+        scale_bc = keep.tile([P, U], F32, name="scale_bc", align_bytes=64)
+        w_codes = keep.tile([P, G, U], U32, name="w_codes", align_bytes=64)
+        w_scales = keep.tile([P, G, U], U8, name="w_scales", align_bytes=64)
+        w2_codes = keep.tile([P, G, A], U32, name="w2_codes", align_bytes=64)
+        w2_scales = keep.tile([P, G, A], U8, name="w2_scales", align_bytes=64)
+        base = keep.tile([P, NT, A], F32, name="base", align_bytes=64)
+        res = keep.tile([P, NT, A], F32, name="res", align_bytes=64)
+        live = {}
+        copy_on = {"V": nc.vector.tensor_copy, "S": nc.scalar.copy}
+
+        def t_SB(s):
+            bank = psum.tile([P, 4, P], F32, name="sbank", tag="xt", bufs=4)
+            for jj in range(4):
+                nc.tensor.transpose(bank[:, jj, :], sc_raw[:, 4 * s + jj : 4 * s + jj + 1].to_broadcast([P, P]), ident[:])
+            copy_on[who["SB", s]](
+                out=scale_bc[:].rearrange("q (p j) -> q p j", j=NB)[:, :, 4 * s : 4 * s + 4],
+                in_=bank[:].rearrange("q j p -> q p j"),
+            )
+
+        def t_I(c, g, s):
+            if s == 0:
+                wg0 = work.tile([P, 512, 4], BF16, name="wg", bufs=4, align_bytes=64)
+                live["wg", c, g] = wg0
+            wg = live["wg", c, g]
+            cols_of = slice(256 * s, 256 * (s + 1))
+            copy_on[who["I", c, g, s]](
+                out=wg[:, cols_of, :].rearrange("p (c i) k -> p c k i", i=4),
+                in_=w_raw[c, g][:, :, cols_of].rearrange("p k (c i) -> p c k i", i=4),
+            )
+
+        def t_QW(c, g):
+            nc.vector.quantize_mx(
+                out=w_codes[:, g, 512 * c : 512 * (c + 1)].bitcast(FP8X4),
+                scales=w_scales[:, g, 512 * c : 512 * (c + 1)],
+                in_=live["wg", c, g][:].rearrange("p n k -> p (n k)"),
+            )
+
+        def t_SC(i):
+            hs = work.tile([P, U], BF16, name="hs", bufs=4, align_bytes=64)
+            nc.vector.tensor_tensor(out=hs[:], in0=h0t[:, i, :].bitcast(FP8), in1=scale_bc[:], op=ALU.mult)
+            live["hs", i] = hs
+
+        def t_HT(i):
+            hg = work.tile([P, G, P, 4], BF16, name="hg", bufs=3, align_bytes=64)
+            words = live["hs", i][:].bitcast(F32)
+            bank = psum.tile([P, G, 2, P], F32, name="hbank", tag="xt", bufs=4)
+            for g in range(G):
+                for u in range(2):
+                    nc.tensor.transpose(bank[:, g, u, :], words[:, 256 * g + u : 256 * (g + 1) : 2], ident[:])
+            copy_on[who["HT", i]](out=hg[:].bitcast(F32), in_=bank[:].rearrange("p g u r -> p g r u"))
+            live["hg", i] = hg
+
+        def t_QH(i):
+            h_codes = work.tile([P, G, P], U32, name="h_codes", bufs=4, align_bytes=64)
+            h_scales = work.tile([P, G, P], U8, name="h_scales", bufs=4, align_bytes=64)
+            nc.vector.quantize_mx(
+                out=h_codes[:].rearrange("p g r -> p (g r)").bitcast(FP8X4),
+                scales=h_scales[:].rearrange("p g r -> p (g r)"),
+                in_=live["hg", i][:].rearrange("p g r t -> p (g r t)"),
+            )
+            live["hq", i] = (h_codes, h_scales)
+
+        def t_B(i, c):
+            if c == 0:
+                v0 = work.tile([P, 2, 4, P], F32, name="v", bufs=8, align_bytes=64)
+                live["v", i] = v0
+            v = live["v", i]
+            h_codes, h_scales = live["hq", i]
+            pre = psum.tile([P, 512], F32, name="pre", tag="pre", bufs=4)
+            for g in range(G):
+                nc.tensor.matmul_mx(
+                    out=pre[:],
+                    lhsT=h_codes[:, g, :].bitcast(FP8X4),
+                    lhsT_scale=h_scales[:, g, :],
+                    rhs=w_codes[:, g, 512 * c : 512 * (c + 1)].bitcast(FP8X4),
+                    rhs_scale=w_scales[:, g, 512 * c : 512 * (c + 1)],
+                    start=(g == 0),
+                    stop=(g == G - 1),
+                )
+            nc.vector.tensor_tensor(
+                out=v[:, c], in0=pre[:].rearrange("p (m t) -> p t m", t=4),
+                in1=b1_bc[:, 512 * c : 512 * (c + 1)].rearrange("p (m t) -> p t m", t=4), op=ALU.add,
+            )
+
+        def t_SG(i):
+            a = work.tile([P, U], F32, name="a", bufs=8, align_bytes=64)
+            nc.scalar.activation(out=a[:], in_=live["v", i][:].rearrange("p c t m -> p (c t m)"), func=ACT.Sigmoid, scale=-1.0)
+            live["a", i] = a
+
+        def t_LN(i):
+            a = live["a", i]
+            nc.scalar.activation(out=a[:], in_=a[:], func=ACT.Ln, bias=tiny_col[:, 0:1])
+
+        def t_TH(i):
+            a = live["a", i]
+            nc.scalar.activation(out=a[:], in_=a[:], func=ACT.Tanh, scale=-1.0)
+
+        def t_M(i):
+            v, a = live["v", i][:].rearrange("p c t m -> p (c t m)"), live["a", i]
+            s1 = work.tile([P, 1], F32, name="s1", bufs=4)
+            nmu = work.tile([P, 1], F32, name="nmu", bufs=8)
+            nc.vector.scalar_tensor_tensor(out=v, in0=v, scalar=1.0, in1=a[:], op0=ALU.mult, op1=ALU.mult, accum_out=s1[:])
+            nc.gpsimd.tensor_scalar(out=nmu[:], in0=s1[:], scalar1=-1.0 / U, scalar2=0.0, op0=ALU.mult, op1=ALU.add)
+            live["nmu", i] = nmu
+
+        def t_SQ(i):
+            v, a, nmu = live["v", i], live["a", i], live["nmu", i]
+            s2 = work.tile([P, 1], F32, name="s2", bufs=4)
+            ve = work.tile([P, 1], F32, name="ve", bufs=4)
+            rstd = work.tile([P, 1], F32, name="rstd", bufs=8)
+            nc.scalar.activation(out=a[:], in_=v[:].rearrange("p c t m -> p (c t m)"), func=ACT.Square, bias=nmu[:], accum_out=s2[:])
+            nc.gpsimd.tensor_scalar(out=ve[:], in0=s2[:], scalar1=1.0 / U, scalar2=EPS, op0=ALU.mult, op1=ALU.add)
+            nc.gpsimd.tensor_tensor(out=rstd[:], in0=ve[:], in1=neg_half[:], op=ALU.pow)
+            live["rstd", i] = rstd
+
+        def t_NR(i):
+            x = work.tile([P, NB, P], F32, name="x", bufs=5, align_bytes=64)
+            nc.vector.tensor_scalar(
+                out=x[:].rearrange("p j m -> p (j m)"), in0=live["v", i][:].rearrange("p c t m -> p (c t m)"),
+                scalar1=live["nmu", i][:], scalar2=live["rstd", i][:], op0=ALU.add, op1=ALU.mult,
+            )
+            live["x", i] = x
+
+        def t_XT(u, b):
+            if b == 0:
+                hp0 = work.tile([P, NB, 256], BF16, name="hp", bufs=2, align_bytes=64)
+                live["hp", u] = hp0
+            hp = live["hp", u]
+            bank = psum.tile([P, 2, 256], F32, name="xbank", tag="xt", bufs=4)
+            for jj in range(2):
+                for e in range(2):
+                    nc.tensor.transpose(bank[:, jj, P * e : P * (e + 1)], live["x", 2 * u + e][:, 2 * b + jj, :], ident[:])
+            for jj in range(2):
+                j = 2 * b + jj
+                if who["XT", u, b] == "S":
+                    nc.scalar.activation(out=hp[:, j, :], in_=bank[:, jj, :], func=ACT.Identity, scale=cols[:, 0, j : j + 1], bias=cols[:, 1, j : j + 1])
+                else:
+                    nc.vector.tensor_scalar(out=hp[:, j, :], in0=bank[:, jj, :], scalar1=cols[:, 0, j : j + 1], scalar2=cols[:, 1, j : j + 1], op0=ALU.mult, op1=ALU.add)
+
+        def t_IL(u):
+            hp = live["hp", u]
+            h1g = work.tile([P, G, 256, 4], BF16, name="h1g", bufs=2, align_bytes=64)
+            for g in range(G):
+                nc.vector.tensor_copy(
+                    out=h1g[:, g].rearrange("p (c i) t -> p c t i", i=4),
+                    in_=hp[:, 4 * g : 4 * g + 4, :].rearrange("p t (c i) -> p c t i", i=4),
+                )
+            live["h1g", u] = h1g
+
+        def t_QX(u):
+            q_codes = work.tile([P, G, 256], U32, name="q_codes", bufs=2, align_bytes=64)
+            q_scales = work.tile([P, G, 256], U8, name="q_scales", bufs=2, align_bytes=64)
+            nc.vector.quantize_mx(
+                out=q_codes[:].rearrange("p g r -> p (g r)").bitcast(FP8X4),
+                scales=q_scales[:].rearrange("p g r -> p (g r)"),
+                in_=live["h1g", u][:].rearrange("p g r t -> p (g r t)"),
+            )
+            live["q", u] = (q_codes, q_scales)
+
+        def t_FN(u):
+            q_codes, q_scales = live["q", u]
+            obank = psum.tile([P, 2, A], F32, name="obank", tag="xt", bufs=4)
+            for e in range(2):
+                for g in range(G):
+                    nc.tensor.matmul_mx(
+                        out=obank[:, e, :],
+                        lhsT=q_codes[:, g, P * e : P * (e + 1)].bitcast(FP8X4),
+                        lhsT_scale=q_scales[:, g, P * e : P * (e + 1)],
+                        rhs=w2_codes[:, g, :].bitcast(FP8X4),
+                        rhs_scale=w2_scales[:, g, :],
+                        start=(g == 0),
+                        stop=(g == G - 1),
+                    )
+            nc.vector.scalar_tensor_tensor(
+                out=res[:, 2 * u : 2 * u + 2, :], in0=obank[:], scalar=0.25, in1=base[:, 2 * u : 2 * u + 2, :], op0=ALU.mult, op1=ALU.add
+            )
+            nc.sync.dma_start(out=out_v[:, 2 * u : 2 * u + 2, :], in_=res[:, 2 * u : 2 * u + 2, :])
+
+        def t_BS(h):
+            bank = psum.tile([P, 4, A], F32, name="bbank", tag="xt", bufs=4)
+            nc.tensor.matmul(out=bank[:], lhsT=quarter_bf[:], rhs=k1_sb[:, 4 * h : 4 * h + 4, :], start=True, stop=False)
+            nc.tensor.matmul(out=bank[:], lhsT=ident_bf[:], rhs=z_sb[:, 4 * h : 4 * h + 4, :], start=False, stop=False)
+            nc.tensor.matmul(out=bank[:], lhsT=ones_bf[:], rhs=b2_bc[:].unsqueeze(1).to_broadcast([P, 4, A]), start=False, stop=True)
+            copy_on[who["BS", h]](out=base[:, 4 * h : 4 * h + 4, :], in_=bank[:])
+
+        def t_W2(g):
+            w2g = work.tile([P, A, 4], BF16, name="w2g", bufs=2, align_bytes=64)
+            copy_on[who["W2", g]](out=w2g[:], in_=w2_raw[:, g].rearrange("p k n -> p n k"))
+            nc.vector.quantize_mx(out=w2_codes[:, g, :].bitcast(FP8X4), scales=w2_scales[:, g, :], in_=w2g[:].rearrange("p n k -> p (n k)"))
+
+        todo = {"SB": t_SB, "I": t_I, "QW": t_QW, "SC": t_SC, "HT": t_HT, "QH": t_QH, "B": t_B, "SG": t_SG, "LN": t_LN, "TH": t_TH, "M": t_M, "SQ": t_SQ, "NR": t_NR, "XT": t_XT, "IL": t_IL, "QX": t_QX, "FN": t_FN, "BS": t_BS, "W2": t_W2}
+        for step in default_order():
+            todo[step[0]](*step[1:])

@@ -33,33 +33,40 @@ def default_who():
             who["I", c, g, 1] = "S"
     for i in range(8):
         who["HT", i] = "S" if i < 4 else "V"
-        who["NR", i] = "V"
-    for u in range(4):
-        for b in range(4):
-            who["XT", u, b] = "V" if u < 2 else "S"
+        who["SQ", i] = "S"
+    for b in range(8):
+        who["XT", 0, b] = "V"
+    for b in range(4):
+        who["XT", 4, b] = "S"
+        who["XT", 6, b] = "S"
     who["SB", 0] = "V"
     who["SB", 1] = "S"
-    for h in range(2):
-        who["BS", h] = "V" if h == 0 else "S"
-        who["W2", h] = "S"
+    who["BS", 0] = who["BS", 1] = "V"
+    who["W2", 0] = "S"
+    who["SQ", 3] = "V"
+    who["I", 0, 1, 0] = "S"
+    who["BS", 0] = "S"
+    who["XT", 4, 3] = "V"
     return who
 
 
 def default_order():
     o = [("SB", 0), ("SB", 1)]
-    o += [("SC", 0), ("I", 0, 0, 0), ("I", 0, 0, 1), ("HT", 0), ("SC", 1), ("I", 0, 1, 0), ("I", 0, 1, 1), ("HT", 1), ("QH", 0), ("SC", 2), ("QW", 0, 0), ("QW", 0, 1), ("HT", 2)]
-    o += [("I", 1, 0, 0), ("I", 1, 0, 1), ("QH", 1), ("SC", 3), ("I", 1, 1, 0), ("I", 1, 1, 1), ("HT", 3), ("QW", 1, 0), ("QH", 2), ("QW", 1, 1)]
-    o += [("B", 0, 0), ("B", 0, 1), ("SG", 0), ("B", 1, 0), ("B", 1, 1), ("SG", 1), ("QH", 3), ("B", 2, 0), ("B", 2, 1), ("SG", 2), ("B", 3, 0), ("B", 3, 1), ("SG", 3)]
-    o += [("LN", i) for i in range(4)]
-    o += [("SC", 4), ("SC", 5), ("HT", 4), ("SC", 6), ("QH", 4), ("HT", 5), ("SC", 7), ("QH", 5), ("HT", 6), ("B", 4, 0), ("B", 4, 1), ("QH", 6), ("HT", 7), ("B", 5, 0), ("QH", 7), ("B", 5, 1)]
-    o += [("TH", 0), ("TH", 1), ("M", 0), ("TH", 2), ("M", 1), ("SG", 4), ("B", 6, 0), ("TH", 3), ("M", 2), ("SQ", 0), ("B", 6, 1), ("SG", 5), ("SQ", 1), ("M", 3), ("SQ", 2), ("B", 7, 0), ("SQ", 3), ("B", 7, 1), ("SG", 6), ("SG", 7)]
-    o += [("NR", 0), ("NR", 1), ("W2", 0), ("W2", 1), ("NR", 2)]
-    o += [("LN", i) for i in range(4, 8)]
-    o += [("XT", 0, b) for b in range(4)] + [("NR", 3), ("IL", 0), ("BS", 0), ("QX", 0)]
-    o += [("XT", 1, b) for b in range(4)] + [("FN", 0), ("IL", 1), ("QX", 1)]
-    o += [("TH", 4), ("TH", 5), ("M", 4), ("TH", 6), ("M", 5), ("SQ", 4), ("TH", 7), ("FN", 1), ("M", 6), ("SQ", 5), ("M", 7), ("SQ", 6), ("BS", 1), ("SQ", 7), ("NR", 4), ("NR", 5), ("NR", 6)]
-    o += [("XT", 2, b) for b in range(4)] + [("NR", 7), ("IL", 2), ("QX", 2)]
-    o += [("XT", 3, b) for b in range(4)] + [("FN", 2), ("IL", 3), ("QX", 3), ("FN", 3)]
+    o += [("I", 0, 0, 0), ("I", 0, 0, 1), ("SC", 0), ("I", 0, 1, 0), ("I", 0, 1, 1), ("SC", 1), ("HT", 0), ("SC", 2), ("HT", 1), ("QW", 0), ("QH", 0)]
+    o += [("I", 1, 0, 0), ("I", 1, 0, 1), ("SC", 3), ("HT", 2), ("I", 1, 1, 0), ("I", 1, 1, 1), ("B", 0, 0), ("HT", 3), ("QW", 1), ("QH", 1)]
+    o += [("W2", 0), ("B", 0, 1), ("BS", 0), ("SG", 0)]
+    for i in range(1, 4):
+        o += [("B", i, 0), ("B", i, 1), ("SG", i)]
+    o += [("LN", 0)]
+    o += [("SC", 4), ("SC", 5), ("HT", 4), ("SC", 6), ("HT", 5), ("QH", 2), ("SC", 7), ("HT", 6), ("HT", 7), ("QH", 3)]
+    o += [("B", 4, 0), ("B", 4, 1), ("B", 5, 0)]
+    o += [("TH", 0), ("M", 0), ("TH", 1), ("B", 5, 1), ("M", 1), ("TH", 2), ("B", 6, 0), ("M", 2), ("TH", 3), ("SG", 4), ("B", 6, 1), ("M", 3), ("SQ", 0), ("SG", 5), ("B", 7, 0), ("B", 7, 1), ("SQ", 1), ("SQ", 2), ("SQ", 3), ("SG", 6), ("SG", 7)]
+    o += [("BS", 1), ("NR", 0), ("NR", 1), ("NR", 2), ("NR", 3)]
+    o += [("LN", 1)]
+    o += [("XT", 0, 4, b) for b in range(8)] + [("IL", 0, 4, 0), ("IL", 0, 4, 1), ("QX", 0, 4)]
+    o += [("TH", 4), ("M", 4), ("FN", 0, 4), ("TH", 5), ("M", 5), ("TH", 6), ("M", 6), ("TH", 7), ("SQ", 4), ("M", 7), ("SQ", 5), ("SQ", 6), ("SQ", 7), ("NR", 4), ("NR", 5)]
+    o += [("XT", 4, 2, 0), ("XT", 4, 2, 1), ("NR", 6), ("NR", 7), ("XT", 4, 2, 2), ("XT", 4, 2, 3), ("XT", 6, 2, 0), ("IL", 4, 2, 0), ("XT", 6, 2, 1), ("IL", 4, 2, 1), ("XT", 6, 2, 2), ("IL", 6, 2, 0), ("XT", 6, 2, 3), ("QX", 4, 2)]
+    o += [("IL", 6, 2, 1), ("FN", 4, 2), ("QX", 6, 2), ("FN", 6, 2)]
     return o
 
 
@@ -95,7 +102,6 @@ def tile_actorflowode_pb_kernel(tc, h0_bytes, h0_scale, z, k1, W1, b1, ln1_g, ln
         nc.sync.dma_start(out=w_raw[1, 0][:], in_=w1v[1, 0])
         nc.sync.dma_start(out=w_raw[1, 1][:], in_=w1v[1, 1])
         nc.sync.dma_start(out=b1_bc[:], in_=b1.partition_broadcast(P))
-        nc.sync.dma_start(out=h0t[:, 4:8, :], in_=h0v[:, 4:8, :])
         cols_bf = []
         for v, vec in enumerate((ln1_g, ln1_b)):
             col_bf = keep.tile([P, NB], BF16, name="col_bf%d" % v)
@@ -111,6 +117,7 @@ def tile_actorflowode_pb_kernel(tc, h0_bytes, h0_scale, z, k1, W1, b1, ln1_g, ln
         w2_raw = keep.tile([P, G, 4, A], BF16, name="w2_raw", align_bytes=64)
         for g in range(G):
             nc.sync.dma_start(out=w2_raw[:, g], in_=W2.rearrange("(g p t) n -> g p t n", p=P, t=4)[g])
+        nc.sync.dma_start(out=h0t[:, 4:8, :], in_=h0v[:, 4:8, :])
         out_v = out.rearrange("(p i) a -> p i a", i=NT)
 
         tiny_col = keep.tile([P, 1], F32, name="tiny_col")
@@ -126,8 +133,8 @@ def tile_actorflowode_pb_kernel(tc, h0_bytes, h0_scale, z, k1, W1, b1, ln1_g, ln
             nc.gpsimd.tensor_scalar(out=cols[:, v, :], in0=cols_bf[v][:], scalar1=1.0, scalar2=0.0, op0=ALU.mult, op1=ALU.add)
 
         scale_bc = keep.tile([P, U], F32, name="scale_bc", align_bytes=64)
-        w_codes = keep.tile([P, G, U], U32, name="w_codes", align_bytes=64)
-        w_scales = keep.tile([P, G, U], U8, name="w_scales", align_bytes=64)
+        w_codes = keep.tile([P, 2, G, 512], U32, name="w_codes", align_bytes=64)
+        w_scales = keep.tile([P, 2, G, 512], U8, name="w_scales", align_bytes=64)
         w2_codes = keep.tile([P, G, A], U32, name="w2_codes", align_bytes=64)
         w2_scales = keep.tile([P, G, A], U8, name="w2_scales", align_bytes=64)
         base = keep.tile([P, NT, A], F32, name="base", align_bytes=64)
@@ -145,21 +152,21 @@ def tile_actorflowode_pb_kernel(tc, h0_bytes, h0_scale, z, k1, W1, b1, ln1_g, ln
             )
 
         def t_I(c, g, s):
-            if s == 0:
-                wg0 = work.tile([P, 512, 4], BF16, name="wg", bufs=4, align_bytes=64)
-                live["wg", c, g] = wg0
-            wg = live["wg", c, g]
+            if (g, s) == (0, 0):
+                wg0 = work.tile([P, G, 512, 4], BF16, name="wg", bufs=2, align_bytes=64)
+                live["wg", c] = wg0
+            wg = live["wg", c][:, g]
             cols_of = slice(256 * s, 256 * (s + 1))
             copy_on[who["I", c, g, s]](
                 out=wg[:, cols_of, :].rearrange("p (c i) k -> p c k i", i=4),
                 in_=w_raw[c, g][:, :, cols_of].rearrange("p k (c i) -> p c k i", i=4),
             )
 
-        def t_QW(c, g):
+        def t_QW(c):
             nc.vector.quantize_mx(
-                out=w_codes[:, g, 512 * c : 512 * (c + 1)].bitcast(FP8X4),
-                scales=w_scales[:, g, 512 * c : 512 * (c + 1)],
-                in_=live["wg", c, g][:].rearrange("p n k -> p (n k)"),
+                out=w_codes[:, c].rearrange("p g n -> p (g n)").bitcast(FP8X4),
+                scales=w_scales[:, c].rearrange("p g n -> p (g n)"),
+                in_=live["wg", c][:].rearrange("p g n k -> p (g n k)"),
             )
 
         def t_SC(i):
@@ -168,39 +175,41 @@ def tile_actorflowode_pb_kernel(tc, h0_bytes, h0_scale, z, k1, W1, b1, ln1_g, ln
             live["hs", i] = hs
 
         def t_HT(i):
-            hg = work.tile([P, G, P, 4], BF16, name="hg", bufs=3, align_bytes=64)
+            if i % 2 == 0:
+                hg0 = work.tile([P, 2, G, P, 4], BF16, name="hg", bufs=3, align_bytes=64)
+                live["hg", i // 2] = hg0
+            hg = live["hg", i // 2][:, i % 2]
             words = live["hs", i][:].bitcast(F32)
             bank = psum.tile([P, G, 2, P], F32, name="hbank", tag="xt", bufs=4)
             for g in range(G):
                 for u in range(2):
                     nc.tensor.transpose(bank[:, g, u, :], words[:, 256 * g + u : 256 * (g + 1) : 2], ident[:])
-            copy_on[who["HT", i]](out=hg[:].bitcast(F32), in_=bank[:].rearrange("p g u r -> p g r u"))
-            live["hg", i] = hg
+            copy_on[who["HT", i]](out=hg.bitcast(F32), in_=bank[:].rearrange("p g u r -> p g r u"))
 
-        def t_QH(i):
-            h_codes = work.tile([P, G, P], U32, name="h_codes", bufs=4, align_bytes=64)
-            h_scales = work.tile([P, G, P], U8, name="h_scales", bufs=4, align_bytes=64)
+        def t_QH(u):
+            h_codes = work.tile([P, 2, G, P], U32, name="h_codes", bufs=4, align_bytes=64)
+            h_scales = work.tile([P, 2, G, P], U8, name="h_scales", bufs=4, align_bytes=64)
             nc.vector.quantize_mx(
-                out=h_codes[:].rearrange("p g r -> p (g r)").bitcast(FP8X4),
-                scales=h_scales[:].rearrange("p g r -> p (g r)"),
-                in_=live["hg", i][:].rearrange("p g r t -> p (g r t)"),
+                out=h_codes[:].rearrange("p e g r -> p (e g r)").bitcast(FP8X4),
+                scales=h_scales[:].rearrange("p e g r -> p (e g r)"),
+                in_=live["hg", u][:].rearrange("p e g r t -> p (e g r t)"),
             )
-            live["hq", i] = (h_codes, h_scales)
+            live["hq", u] = (h_codes, h_scales)
 
         def t_B(i, c):
             if c == 0:
                 v0 = work.tile([P, 2, 4, P], F32, name="v", bufs=8, align_bytes=64)
                 live["v", i] = v0
             v = live["v", i]
-            h_codes, h_scales = live["hq", i]
+            h_codes, h_scales = live["hq", i // 2]
             pre = psum.tile([P, 512], F32, name="pre", tag="pre", bufs=4)
             for g in range(G):
                 nc.tensor.matmul_mx(
                     out=pre[:],
-                    lhsT=h_codes[:, g, :].bitcast(FP8X4),
-                    lhsT_scale=h_scales[:, g, :],
-                    rhs=w_codes[:, g, 512 * c : 512 * (c + 1)].bitcast(FP8X4),
-                    rhs_scale=w_scales[:, g, 512 * c : 512 * (c + 1)],
+                    lhsT=h_codes[:, i % 2, g, :].bitcast(FP8X4),
+                    lhsT_scale=h_scales[:, i % 2, g, :],
+                    rhs=w_codes[:, c, g, :].bitcast(FP8X4),
+                    rhs_scale=w_scales[:, c, g, :],
                     start=(g == 0),
                     stop=(g == G - 1),
                 )
@@ -210,32 +219,37 @@ def tile_actorflowode_pb_kernel(tc, h0_bytes, h0_scale, z, k1, W1, b1, ln1_g, ln
             )
 
         def t_SG(i):
-            a = work.tile([P, U], F32, name="a", bufs=8, align_bytes=64)
-            nc.scalar.activation(out=a[:], in_=live["v", i][:].rearrange("p c t m -> p (c t m)"), func=ACT.Sigmoid, scale=-1.0)
-            live["a", i] = a
+            if i % 4 == 0:
+                a0 = work.tile([P, 4, U], F32, name="a", bufs=2, align_bytes=64)
+                live["a", i // 4] = a0
+            nc.scalar.activation(out=live["a", i // 4][:, i % 4], in_=live["v", i][:].rearrange("p c t m -> p (c t m)"), func=ACT.Sigmoid, scale=-1.0)
 
-        def t_LN(i):
-            a = live["a", i]
-            nc.scalar.activation(out=a[:], in_=a[:], func=ACT.Ln, bias=tiny_col[:, 0:1])
+        def t_LN(h):
+            a = live["a", h][:].rearrange("p i n -> p (i n)")
+            nc.scalar.activation(out=a, in_=a, func=ACT.Ln, bias=tiny_col[:, 0:1])
 
         def t_TH(i):
-            a = live["a", i]
-            nc.scalar.activation(out=a[:], in_=a[:], func=ACT.Tanh, scale=-1.0)
+            a = live["a", i // 4][:, i % 4]
+            nc.scalar.activation(out=a, in_=a, func=ACT.Tanh, scale=-1.0)
 
         def t_M(i):
-            v, a = live["v", i][:].rearrange("p c t m -> p (c t m)"), live["a", i]
+            v, a = live["v", i][:].rearrange("p c t m -> p (c t m)"), live["a", i // 4][:, i % 4]
             s1 = work.tile([P, 1], F32, name="s1", bufs=4)
             nmu = work.tile([P, 1], F32, name="nmu", bufs=8)
-            nc.vector.scalar_tensor_tensor(out=v, in0=v, scalar=1.0, in1=a[:], op0=ALU.mult, op1=ALU.mult, accum_out=s1[:])
+            nc.vector.scalar_tensor_tensor(out=v, in0=v, scalar=1.0, in1=a, op0=ALU.mult, op1=ALU.mult, accum_out=s1[:])
             nc.gpsimd.tensor_scalar(out=nmu[:], in0=s1[:], scalar1=-1.0 / U, scalar2=0.0, op0=ALU.mult, op1=ALU.add)
             live["nmu", i] = nmu
 
         def t_SQ(i):
-            v, a, nmu = live["v", i], live["a", i], live["nmu", i]
+            v, a, nmu = live["v", i], live["a", i // 4][:, i % 4], live["nmu", i]
             s2 = work.tile([P, 1], F32, name="s2", bufs=4)
             ve = work.tile([P, 1], F32, name="ve", bufs=4)
             rstd = work.tile([P, 1], F32, name="rstd", bufs=8)
-            nc.scalar.activation(out=a[:], in_=v[:].rearrange("p c t m -> p (c t m)"), func=ACT.Square, bias=nmu[:], accum_out=s2[:])
+            vf = v[:].rearrange("p c t m -> p (c t m)")
+            if who.get(("SQ", i), "S") == "S":
+                nc.scalar.activation(out=a, in_=vf, func=ACT.Square, bias=nmu[:], accum_out=s2[:])
+            else:
+                nc.vector.scalar_tensor_tensor(out=a, in0=vf, scalar=nmu[:], in1=vf, op0=ALU.add, op1=ALU.mult, accum_out=s2[:])
             nc.gpsimd.tensor_scalar(out=ve[:], in0=s2[:], scalar1=1.0 / U, scalar2=EPS, op0=ALU.mult, op1=ALU.add)
             nc.gpsimd.tensor_tensor(out=rstd[:], in0=ve[:], in1=neg_half[:], op=ALU.pow)
             live["rstd", i] = rstd
@@ -248,46 +262,46 @@ def tile_actorflowode_pb_kernel(tc, h0_bytes, h0_scale, z, k1, W1, b1, ln1_g, ln
             )
             live["x", i] = x
 
-        def t_XT(u, b):
+        def t_XT(first, n, b):
+            per = 4 // n
             if b == 0:
-                hp0 = work.tile([P, NB, 256], BF16, name="hp", bufs=2, align_bytes=64)
-                live["hp", u] = hp0
-            hp = live["hp", u]
-            bank = psum.tile([P, 2, 256], F32, name="xbank", tag="xt", bufs=4)
-            for jj in range(2):
-                for e in range(2):
-                    nc.tensor.transpose(bank[:, jj, P * e : P * (e + 1)], live["x", 2 * u + e][:, 2 * b + jj, :], ident[:])
-            for jj in range(2):
-                j = 2 * b + jj
-                if who["XT", u, b] == "S":
+                hp0 = work.tile([P, NB, P * n], BF16, name="hp%d" % n, bufs=3 - n // 2, align_bytes=64)
+                live["hp", first] = hp0
+            hp = live["hp", first]
+            bank = psum.tile([P, per, P * n], F32, name="xbank", tag="xt", bufs=4)
+            for jj in range(per):
+                for e in range(n):
+                    nc.tensor.transpose(bank[:, jj, P * e : P * (e + 1)], live["x", first + e][:, per * b + jj, :], ident[:])
+            for jj in range(per):
+                j = per * b + jj
+                if who["XT", first, b] == "S":
                     nc.scalar.activation(out=hp[:, j, :], in_=bank[:, jj, :], func=ACT.Identity, scale=cols[:, 0, j : j + 1], bias=cols[:, 1, j : j + 1])
                 else:
                     nc.vector.tensor_scalar(out=hp[:, j, :], in0=bank[:, jj, :], scalar1=cols[:, 0, j : j + 1], scalar2=cols[:, 1, j : j + 1], op0=ALU.mult, op1=ALU.add)
 
-        def t_IL(u):
-            hp = live["hp", u]
-            h1g = work.tile([P, G, 256, 4], BF16, name="h1g", bufs=2, align_bytes=64)
-            for g in range(G):
-                nc.vector.tensor_copy(
-                    out=h1g[:, g].rearrange("p (c i) t -> p c t i", i=4),
-                    in_=hp[:, 4 * g : 4 * g + 4, :].rearrange("p t (c i) -> p c t i", i=4),
-                )
-            live["h1g", u] = h1g
+        def t_IL(first, n, g):
+            if g == 0:
+                h1g0 = work.tile([P, G, P * n, 4], BF16, name="h1g%d" % n, bufs=3 - n // 2, align_bytes=64)
+                live["h1g", first] = h1g0
+            nc.vector.tensor_copy(
+                out=live["h1g", first][:, g].rearrange("p (c i) t -> p c t i", i=4),
+                in_=live["hp", first][:, 4 * g : 4 * g + 4, :].rearrange("p t (c i) -> p c t i", i=4),
+            )
 
-        def t_QX(u):
-            q_codes = work.tile([P, G, 256], U32, name="q_codes", bufs=2, align_bytes=64)
-            q_scales = work.tile([P, G, 256], U8, name="q_scales", bufs=2, align_bytes=64)
+        def t_QX(first, n):
+            q_codes = work.tile([P, G, P * n], U32, name="q_codes%d" % n, bufs=3 - n // 2, align_bytes=64)
+            q_scales = work.tile([P, G, P * n], U8, name="q_scales%d" % n, bufs=3 - n // 2, align_bytes=64)
             nc.vector.quantize_mx(
                 out=q_codes[:].rearrange("p g r -> p (g r)").bitcast(FP8X4),
                 scales=q_scales[:].rearrange("p g r -> p (g r)"),
-                in_=live["h1g", u][:].rearrange("p g r t -> p (g r t)"),
+                in_=live["h1g", first][:].rearrange("p g r t -> p (g r t)"),
             )
-            live["q", u] = (q_codes, q_scales)
+            live["q", first] = (q_codes, q_scales)
 
-        def t_FN(u):
-            q_codes, q_scales = live["q", u]
-            obank = psum.tile([P, 2, A], F32, name="obank", tag="xt", bufs=4)
-            for e in range(2):
+        def t_FN(first, n):
+            q_codes, q_scales = live["q", first]
+            obank = psum.tile([P, n, A], F32, name="obank", tag="xt", bufs=4)
+            for e in range(n):
                 for g in range(G):
                     nc.tensor.matmul_mx(
                         out=obank[:, e, :],
@@ -298,10 +312,9 @@ def tile_actorflowode_pb_kernel(tc, h0_bytes, h0_scale, z, k1, W1, b1, ln1_g, ln
                         start=(g == 0),
                         stop=(g == G - 1),
                     )
-            nc.vector.scalar_tensor_tensor(
-                out=res[:, 2 * u : 2 * u + 2, :], in0=obank[:], scalar=0.25, in1=base[:, 2 * u : 2 * u + 2, :], op0=ALU.mult, op1=ALU.add
-            )
-            nc.sync.dma_start(out=out_v[:, 2 * u : 2 * u + 2, :], in_=res[:, 2 * u : 2 * u + 2, :])
+            rows = slice(first, first + n)
+            nc.vector.scalar_tensor_tensor(out=res[:, rows, :], in0=obank[:], scalar=0.25, in1=base[:, rows, :], op0=ALU.mult, op1=ALU.add)
+            nc.sync.dma_start(out=out_v[:, rows, :], in_=res[:, rows, :])
 
         def t_BS(h):
             bank = psum.tile([P, 4, A], F32, name="bbank", tag="xt", bufs=4)
@@ -310,10 +323,15 @@ def tile_actorflowode_pb_kernel(tc, h0_bytes, h0_scale, z, k1, W1, b1, ln1_g, ln
             nc.tensor.matmul(out=bank[:], lhsT=ones_bf[:], rhs=b2_bc[:].unsqueeze(1).to_broadcast([P, 4, A]), start=False, stop=True)
             copy_on[who["BS", h]](out=base[:, 4 * h : 4 * h + 4, :], in_=bank[:])
 
-        def t_W2(g):
-            w2g = work.tile([P, A, 4], BF16, name="w2g", bufs=2, align_bytes=64)
-            copy_on[who["W2", g]](out=w2g[:], in_=w2_raw[:, g].rearrange("p k n -> p n k"))
-            nc.vector.quantize_mx(out=w2_codes[:, g, :].bitcast(FP8X4), scales=w2_scales[:, g, :], in_=w2g[:].rearrange("p n k -> p (n k)"))
+        def t_W2(z0):
+            w2g = work.tile([P, G, A, 4], BF16, name="w2g", bufs=1, align_bytes=64)
+            for g in range(G):
+                copy_on[who["W2", 0]](out=w2g[:, g], in_=w2_raw[:, g].rearrange("p k n -> p n k"))
+            nc.vector.quantize_mx(
+                out=w2_codes[:].rearrange("p g n -> p (g n)").bitcast(FP8X4),
+                scales=w2_scales[:].rearrange("p g n -> p (g n)"),
+                in_=w2g[:].rearrange("p g n k -> p (g n k)"),
+            )
 
         todo = {"SB": t_SB, "I": t_I, "QW": t_QW, "SC": t_SC, "HT": t_HT, "QH": t_QH, "B": t_B, "SG": t_SG, "LN": t_LN, "TH": t_TH, "M": t_M, "SQ": t_SQ, "NR": t_NR, "XT": t_XT, "IL": t_IL, "QX": t_QX, "FN": t_FN, "BS": t_BS, "W2": t_W2}
         for step in default_order():

@@ -43,30 +43,38 @@ def default_who():
     who["SB", 1] = "S"
     who["BS", 0] = who["BS", 1] = "V"
     who["W2", 0] = "S"
-    who["SQ", 3] = "V"
     who["I", 0, 1, 0] = "S"
-    who["BS", 0] = "S"
-    who["XT", 4, 3] = "V"
+    who["I", 1, 0, 0] = "V"
+    who["I", 1, 1, 1] = "S"
+    who["SQ", 1] = "V"
+    who["SQ", 3] = "V"
+    who["SQ", 6] = "S"
+    who["W2", 0] = "S"
+    who["BS", 0] = "V"
+    who["XT", 0, 6] = "V"
+    who["XT", 0, 7] = "V"
+    who["XT", 4, 2] = "V"
+    who["BS", 1] = "S"
     return who
 
 
 def default_order():
     o = [("SB", 0), ("SB", 1)]
     o += [("I", 0, 0, 0), ("I", 0, 0, 1), ("SC", 0), ("I", 0, 1, 0), ("I", 0, 1, 1), ("SC", 1), ("HT", 0), ("SC", 2), ("HT", 1), ("QW", 0), ("QH", 0)]
-    o += [("I", 1, 0, 0), ("I", 1, 0, 1), ("SC", 3), ("HT", 2), ("I", 1, 1, 0), ("I", 1, 1, 1), ("B", 0, 0), ("HT", 3), ("QW", 1), ("QH", 1)]
-    o += [("W2", 0), ("B", 0, 1), ("BS", 0), ("SG", 0)]
-    for i in range(1, 4):
-        o += [("B", i, 0), ("B", i, 1), ("SG", i)]
+    o += [("I", 1, 0, 0), ("I", 1, 0, 1), ("SC", 3), ("HT", 2), ("B", 0, 0), ("B", 1, 0), ("I", 1, 1, 0), ("I", 1, 1, 1), ("HT", 3), ("SG", 0, 0), ("QH", 1), ("QW", 1), ("SG", 1, 0), ("B", 2, 0), ("B", 3, 0), ("SG", 2, 0), ("SG", 3, 0)]
+    for i in range(4):
+        o += [("B", i, 1), ("SG", i, 1)]
     o += [("LN", 0)]
     o += [("SC", 4), ("SC", 5), ("HT", 4), ("SC", 6), ("HT", 5), ("QH", 2), ("SC", 7), ("HT", 6), ("HT", 7), ("QH", 3)]
-    o += [("B", 4, 0), ("B", 4, 1), ("B", 5, 0)]
-    o += [("TH", 0), ("M", 0), ("TH", 1), ("B", 5, 1), ("M", 1), ("TH", 2), ("B", 6, 0), ("M", 2), ("TH", 3), ("SG", 4), ("B", 6, 1), ("M", 3), ("SQ", 0), ("SG", 5), ("B", 7, 0), ("B", 7, 1), ("SQ", 1), ("SQ", 2), ("SQ", 3), ("SG", 6), ("SG", 7)]
-    o += [("BS", 1), ("NR", 0), ("NR", 1), ("NR", 2), ("NR", 3)]
-    o += [("LN", 1)]
+    o += [("TH", 0), ("B", 4, 0), ("B", 4, 1), ("M", 0)]
+    for i in range(1, 4):
+        o += [("TH", i), ("B", 4 + i, 0), ("M", i), ("B", 4 + i, 1)]
+    o += [("SG", 4), ("SQ", 0), ("SG", 5), ("SQ", 2), ("SG", 6), ("SG", 7), ("LN", 1)]
+    o += [("RS", 0, True), ("SQ", 1), ("RS", 2, True), ("SQ", 3), ("RS", 1, True), ("BS", 0), ("RS", 3, True), ("NR", 0), ("NR", 2), ("NR", 1), ("NR", 3)]
     o += [("XT", 0, 4, b) for b in range(8)] + [("IL", 0, 4, 0), ("IL", 0, 4, 1), ("QX", 0, 4)]
-    o += [("TH", 4), ("M", 4), ("FN", 0, 4), ("TH", 5), ("M", 5), ("TH", 6), ("M", 6), ("TH", 7), ("SQ", 4), ("M", 7), ("SQ", 5), ("SQ", 6), ("SQ", 7), ("NR", 4), ("NR", 5)]
-    o += [("XT", 4, 2, 0), ("XT", 4, 2, 1), ("NR", 6), ("NR", 7), ("XT", 4, 2, 2), ("XT", 4, 2, 3), ("XT", 6, 2, 0), ("IL", 4, 2, 0), ("XT", 6, 2, 1), ("IL", 4, 2, 1), ("XT", 6, 2, 2), ("IL", 6, 2, 0), ("XT", 6, 2, 3), ("QX", 4, 2)]
-    o += [("IL", 6, 2, 1), ("FN", 4, 2), ("QX", 6, 2), ("FN", 6, 2)]
+    o += [("TH", 4), ("TH", 5), ("M", 4), ("TH", 6), ("M", 5), ("TH", 7), ("W2", 0), ("BS", 1), ("SQ", 4), ("M", 6), ("SQ", 5), ("RS", 4, True), ("M", 7), ("RS", 5, True), ("FN", 0, 4), ("SQ", 6), ("RS", 6, True), ("NR", 4), ("SQ", 7), ("NR", 5), ("RS", 7, True), ("NR", 6)]
+    o += [("XT", 4, 2, b) for b in range(3)] + [("NR", 7), ("XT", 4, 2, 3)]
+    o += [("XT", 6, 2, 0), ("IL", 4, 2, 0), ("XT", 6, 2, 1), ("IL", 4, 2, 1), ("XT", 6, 2, 2), ("QX", 4, 2), ("IL", 6, 2, 0), ("XT", 6, 2, 3), ("IL", 6, 2, 1), ("QX", 6, 2), ("FN", 4, 2), ("FN", 6, 2)]
     return o
 
 
@@ -102,6 +110,7 @@ def tile_actorflowode_pb_kernel(tc, h0_bytes, h0_scale, z, k1, W1, b1, ln1_g, ln
         nc.sync.dma_start(out=w_raw[1, 0][:], in_=w1v[1, 0])
         nc.sync.dma_start(out=w_raw[1, 1][:], in_=w1v[1, 1])
         nc.sync.dma_start(out=b1_bc[:], in_=b1.partition_broadcast(P))
+        nc.sync.dma_start(out=h0t[:, 4:8, :], in_=h0v[:, 4:8, :])
         cols_bf = []
         for v, vec in enumerate((ln1_g, ln1_b)):
             col_bf = keep.tile([P, NB], BF16, name="col_bf%d" % v)
@@ -117,7 +126,6 @@ def tile_actorflowode_pb_kernel(tc, h0_bytes, h0_scale, z, k1, W1, b1, ln1_g, ln
         w2_raw = keep.tile([P, G, 4, A], BF16, name="w2_raw", align_bytes=64)
         for g in range(G):
             nc.sync.dma_start(out=w2_raw[:, g], in_=W2.rearrange("(g p t) n -> g p t n", p=P, t=4)[g])
-        nc.sync.dma_start(out=h0t[:, 4:8, :], in_=h0v[:, 4:8, :])
         out_v = out.rearrange("(p i) a -> p i a", i=NT)
 
         tiny_col = keep.tile([P, 1], F32, name="tiny_col")
@@ -218,39 +226,50 @@ def tile_actorflowode_pb_kernel(tc, h0_bytes, h0_scale, z, k1, W1, b1, ln1_g, ln
                 in1=b1_bc[:, 512 * c : 512 * (c + 1)].rearrange("p (m t) -> p t m", t=4), op=ALU.add,
             )
 
-        def t_SG(i):
-            if i % 4 == 0:
-                a0 = work.tile([P, 4, U], F32, name="a", bufs=2, align_bytes=64)
-                live["a", i // 4] = a0
-            nc.scalar.activation(out=live["a", i // 4][:, i % 4], in_=live["v", i][:].rearrange("p c t m -> p (c t m)"), func=ACT.Sigmoid, scale=-1.0)
+        def t_SG(i, c=None):
+            if i // 4 not in live.setdefault("a", {}):
+                a0 = work.tile([P, 4, 2, 512], F32, name="a", bufs=2, align_bytes=64)
+                live["a"][i // 4] = a0
+            a = live["a"][i // 4][:, i % 4]
+            half = slice(0, 2) if c is None else slice(c, c + 1)
+            nc.scalar.activation(
+                out=a[:, half].rearrange("p c n -> p (c n)"),
+                in_=live["v", i][:, half].rearrange("p c t m -> p (c t m)"), func=ACT.Sigmoid, scale=-1.0,
+            )
 
         def t_LN(h):
-            a = live["a", h][:].rearrange("p i n -> p (i n)")
+            a = live["a"][h][:].rearrange("p i c n -> p (i c n)")
             nc.scalar.activation(out=a, in_=a, func=ACT.Ln, bias=tiny_col[:, 0:1])
 
         def t_TH(i):
-            a = live["a", i // 4][:, i % 4]
+            a = live["a"][i // 4][:, i % 4].rearrange("p c n -> p (c n)")
             nc.scalar.activation(out=a, in_=a, func=ACT.Tanh, scale=-1.0)
 
         def t_M(i):
-            v, a = live["v", i][:].rearrange("p c t m -> p (c t m)"), live["a", i // 4][:, i % 4]
-            s1 = work.tile([P, 1], F32, name="s1", bufs=4)
-            nmu = work.tile([P, 1], F32, name="nmu", bufs=8)
+            v, a = live["v", i][:].rearrange("p c t m -> p (c t m)"), live["a"][i // 4][:, i % 4].rearrange("p c n -> p (c n)")
+            s1 = work.tile([P, 1], F32, name="s1", bufs=8)
+            mean = work.tile([P, 1], F32, name="mean", bufs=8)
             nc.vector.scalar_tensor_tensor(out=v, in0=v, scalar=1.0, in1=a, op0=ALU.mult, op1=ALU.mult, accum_out=s1[:])
-            nc.gpsimd.tensor_scalar(out=nmu[:], in0=s1[:], scalar1=-1.0 / U, scalar2=0.0, op0=ALU.mult, op1=ALU.add)
-            live["nmu", i] = nmu
+            nc.gpsimd.tensor_scalar(out=mean[:], in0=s1[:], scalar1=1.0 / U, scalar2=0.0, op0=ALU.mult, op1=ALU.add)
+            live["s1", i] = s1
+            live["mean", i] = mean
 
         def t_SQ(i):
-            v, a, nmu = live["v", i], live["a", i // 4][:, i % 4], live["nmu", i]
-            s2 = work.tile([P, 1], F32, name="s2", bufs=4)
-            ve = work.tile([P, 1], F32, name="ve", bufs=4)
-            rstd = work.tile([P, 1], F32, name="rstd", bufs=8)
-            vf = v[:].rearrange("p c t m -> p (c t m)")
-            if who.get(("SQ", i), "S") == "S":
-                nc.scalar.activation(out=a, in_=vf, func=ACT.Square, bias=nmu[:], accum_out=s2[:])
+            v, a = live["v", i][:].rearrange("p c t m -> p (c t m)"), live["a"][i // 4][:, i % 4].rearrange("p c n -> p (c n)")
+            s2 = work.tile([P, 1], F32, name="s2", bufs=8)
+            if who["SQ", i] == "S":
+                nc.scalar.activation(out=a, in_=v, func=ACT.Square, scale=-1.0 * U, bias=live["s1", i][:], accum_out=s2[:])
+                live["s2", i] = (s2, 1.0 / U**3)
             else:
-                nc.vector.scalar_tensor_tensor(out=a, in0=vf, scalar=nmu[:], in1=vf, op0=ALU.add, op1=ALU.mult, accum_out=s2[:])
-            nc.gpsimd.tensor_scalar(out=ve[:], in0=s2[:], scalar1=1.0 / U, scalar2=EPS, op0=ALU.mult, op1=ALU.add)
+                nc.vector.scalar_tensor_tensor(out=a, in0=v, scalar=live["mean", i][:], in1=v, op0=ALU.subtract, op1=ALU.mult, accum_out=s2[:])
+                live["s2", i] = (s2, 1.0 / U)
+
+        def t_RS(i, on_vector):
+            s2, factor = live["s2", i]
+            ve = work.tile([P, 1], F32, name="ve", bufs=8)
+            rstd = work.tile([P, 1], F32, name="rstd", bufs=8)
+            engine = nc.vector if on_vector else nc.gpsimd
+            engine.tensor_scalar(out=ve[:], in0=s2[:], scalar1=factor, scalar2=EPS, op0=ALU.mult, op1=ALU.add)
             nc.gpsimd.tensor_tensor(out=rstd[:], in0=ve[:], in1=neg_half[:], op=ALU.pow)
             live["rstd", i] = rstd
 
@@ -258,7 +277,7 @@ def tile_actorflowode_pb_kernel(tc, h0_bytes, h0_scale, z, k1, W1, b1, ln1_g, ln
             x = work.tile([P, NB, P], F32, name="x", bufs=5, align_bytes=64)
             nc.vector.tensor_scalar(
                 out=x[:].rearrange("p j m -> p (j m)"), in0=live["v", i][:].rearrange("p c t m -> p (c t m)"),
-                scalar1=live["nmu", i][:], scalar2=live["rstd", i][:], op0=ALU.add, op1=ALU.mult,
+                scalar1=live["mean", i][:], scalar2=live["rstd", i][:], op0=ALU.subtract, op1=ALU.mult,
             )
             live["x", i] = x
 
@@ -316,6 +335,11 @@ def tile_actorflowode_pb_kernel(tc, h0_bytes, h0_scale, z, k1, W1, b1, ln1_g, ln
             nc.vector.scalar_tensor_tensor(out=res[:, rows, :], in0=obank[:], scalar=0.25, in1=base[:, rows, :], op0=ALU.mult, op1=ALU.add)
             nc.sync.dma_start(out=out_v[:, rows, :], in_=res[:, rows, :])
 
+        def t_WU(n):
+            wbank = psum.tile([P, 512], F32, name="wbank", tag="xt", bufs=4)
+            for k in range(n):
+                nc.tensor.matmul(out=wbank[:], lhsT=ident_bf[:], rhs=w_raw[0, 0][:, k % 4, :], start=(k == 0), stop=(k == n - 1))
+
         def t_BS(h):
             bank = psum.tile([P, 4, A], F32, name="bbank", tag="xt", bufs=4)
             nc.tensor.matmul(out=bank[:], lhsT=quarter_bf[:], rhs=k1_sb[:, 4 * h : 4 * h + 4, :], start=True, stop=False)
@@ -333,6 +357,6 @@ def tile_actorflowode_pb_kernel(tc, h0_bytes, h0_scale, z, k1, W1, b1, ln1_g, ln
                 in_=w2g[:].rearrange("p g n k -> p (g n k)"),
             )
 
-        todo = {"SB": t_SB, "I": t_I, "QW": t_QW, "SC": t_SC, "HT": t_HT, "QH": t_QH, "B": t_B, "SG": t_SG, "LN": t_LN, "TH": t_TH, "M": t_M, "SQ": t_SQ, "NR": t_NR, "XT": t_XT, "IL": t_IL, "QX": t_QX, "FN": t_FN, "BS": t_BS, "W2": t_W2}
+        todo = {"SB": t_SB, "I": t_I, "QW": t_QW, "SC": t_SC, "HT": t_HT, "QH": t_QH, "B": t_B, "SG": t_SG, "LN": t_LN, "TH": t_TH, "M": t_M, "SQ": t_SQ, "NR": t_NR, "RS": t_RS, "XT": t_XT, "IL": t_IL, "QX": t_QX, "FN": t_FN, "BS": t_BS, "WU": t_WU, "W2": t_W2}
         for step in default_order():
             todo[step[0]](*step[1:])

from contextlib import ExitStack

import concourse.mybir as mybir
from concourse.masks import make_identity

F32 = mybir.dt.float32
BF16 = mybir.dt.bfloat16
U32 = mybir.dt.uint32
U8 = mybir.dt.uint8
FP8 = mybir.dt.float8_e4m3fn
FP8X4 = mybir.dt.float8_e4m3fn_x4
ALU = mybir.AluOpType
ACT = mybir.ActivationFunctionType

P = 128
B = 1024
U = 1024
A = 128
G = 2
NB = 8
NT = 8
EPS = 1e-5
TINY = 1e-15

FLOPS = 2 * B * U * U + 2 * B * U * A


def default_who():
    who = {}
    for c in range(2):
        for g in range(2):
            who["I", c, g, 0] = "V"
            who["I", c, g, 1] = "S"
    for i in range(8):
        who["HT", i] = "S" if i < 4 else "V"
        who["SQ", i] = "S"
    for b in range(8):
        who["XT", 0, b] = "V"
    for b in range(4):
        who["XT", 4, b] = "S"
        who["XT", 6, b] = "S"
    who["SB", 0] = "V"
    who["SB", 1] = "S"
    who["BS", 0] = who["BS", 1] = "V"
    who["W2", 0] = "S"
    who["I", 0, 1, 0] = "S"
    who["I", 1, 0, 0] = "V"
    who["I", 1, 1, 1] = "S"
    who["SQ", 1] = "V"
    who["SQ", 3] = "V"
    who["SQ", 6] = "S"
    who["W2", 0] = "S"
    who["BS", 0] = "V"
    who["XT", 0, 6] = "V"
    who["XT", 0, 7] = "V"
    who["XT", 4, 2] = "V"
    who["BS", 1] = "S"
    return who


def default_order():
    o = [("SB", 0), ("SB", 1)]
    o += [("I", 0, 0, 0), ("I", 0, 0, 1), ("SC", 0), ("I", 0, 1, 0), ("I", 0, 1, 1), ("SC", 1), ("HT", 0), ("SC", 2), ("HT", 1), ("QW", 0), ("QH", 0)]
    o += [("I", 1, 0, 0), ("I", 1, 0, 1), ("SC", 3), ("HT", 2), ("B", 0, 0), ("B", 1, 0), ("I", 1, 1, 0), ("I", 1, 1, 1), ("HT", 3), ("SG", 0, 0), ("QH", 1), ("QW", 1), ("SG", 1, 0), ("B", 2, 0), ("B", 3, 0), ("SG", 2, 0), ("SG", 3, 0)]
    for i in range(4):
        o += [("B", i, 1), ("SG", i, 1)]
    o += [("LN", 0)]
    o += [("SC", 4), ("SC", 5), ("HT", 4), ("SC", 6), ("HT", 5), ("QH", 2), ("SC", 7), ("HT", 6), ("HT", 7), ("QH", 3)]
    o += [("TH", 0), ("B", 4, 0), ("B", 4, 1), ("M", 0)]
    for i in range(1, 4):
        o += [("TH", i), ("B", 4 + i, 0), ("M", i), ("B", 4 + i, 1)]
    o += [("SG", 4), ("SQ", 0), ("SG", 5), ("SQ", 2), ("SG", 6), ("SG", 7), ("LN", 1)]
    o += [("RS", 0, True), ("SQ", 1), ("RS", 2, True), ("SQ", 3), ("RS", 1, True), ("BS", 0), ("RS", 3, True), ("NR", 0), ("NR", 2), ("NR", 1), ("NR", 3)]
    o += [("XT", 0, 4, b) for b in range(8)] + [("IL", 0, 4, 0), ("IL", 0, 4, 1), ("QX", 0, 4)]
    o += [("TH", 4), ("TH", 5), ("M", 4), ("TH", 6), ("M", 5), ("TH", 7), ("W2", 0), ("BS", 1), ("SQ", 4), ("M", 6), ("SQ", 5), ("RS", 4, True), ("M", 7), ("RS", 5, True), ("FN", 0, 4), ("SQ", 6), ("RS", 6, True), ("NR", 4), ("SQ", 7), ("NR", 5), ("RS", 7, True), ("NR", 6)]
    o += [("XT", 4, 2, b) for b in range(3)] + [("NR", 7), ("XT", 4, 2, 3)]
    o += [("XT", 6, 2, 0), ("IL", 4, 2, 0), ("XT", 6, 2, 1), ("IL", 4, 2, 1), ("XT", 6, 2, 2), ("QX", 4, 2), ("IL", 6, 2, 0), ("XT", 6, 2, 3), ("IL", 6, 2, 1), ("QX", 6, 2), ("FN", 4, 2), ("FN", 6, 2)]
    return o


def tile_actorflowode_pb_kernel(tc, h0_bytes, h0_scale, z, k1, W1, b1, ln1_g, ln1_b, W2, b2, out):
    nc = tc.nc
    who = default_who()
    with ExitStack() as ctx:
        keep = ctx.enter_context(tc.tile_pool(name="keep", bufs=1))
        work = ctx.enter_context(tc.tile_pool(name="work", bufs=2))
        psum = ctx.enter_context(tc.psum_pool(name="psum", bufs=2))
        ctx.enter_context(tc.manual_schedule(engines={mybir.EngineType.Activation, mybir.EngineType.DVE, mybir.EngineType.PE, mybir.EngineType.SP, mybir.EngineType.Pool}))

        h0t = keep.tile([P, NT, U], U8, name="h0t", align_bytes=64)
        h0v = h0_bytes.rearrange("(p i) k -> p i k", i=NT)
        sc_raw = keep.tile([P, NB], F32, name="sc_raw")
        b1_bc = keep.tile([P, U], BF16, name="b1_bc", align_bytes=64)
        neg_half = keep.tile([P, 1], F32, name="neg_half")
        warm = keep.tile([P, 1], F32, name="warm")
        ident = keep.tile([P, P], F32, name="ident")
        w1v = W1.rearrange("(g p t) (c n) -> c g p t n", p=P, t=4, c=2)
        w_raw = {}
        for c in range(2):
            for g in range(G):
                w_raw[c, g] = keep.tile([P, 4, 512], BF16, name="w_raw%d%d" % (c, g), align_bytes=64)
        nc.sync.dma_start(out=sc_raw[:], in_=h0_scale.rearrange("o (p j) -> (o p) j", j=NB))
        nc.gpsimd.memset(neg_half[:], -0.5)
        make_identity(nc, ident[:])
        nc.sync.dma_start(out=h0t[:, 0:2, :], in_=h0v[:, 0:2, :])
        nc.scalar.activation(out=warm[:], in_=neg_half[:], func=ACT.Sigmoid)
        nc.sync.dma_start(out=w_raw[0, 0][:], in_=w1v[0, 0])
        nc.sync.dma_start(out=w_raw[0, 1][:], in_=w1v[0, 1])
        nc.sync.dma_start(out=h0t[:, 2:4, :], in_=h0v[:, 2:4, :])
        nc.sync.dma_start(out=w_raw[1, 0][:], in_=w1v[1, 0])
        nc.sync.dma_start(out=w_raw[1, 1][:], in_=w1v[1, 1])
        nc.sync.dma_start(out=b1_bc[:], in_=b1.partition_broadcast(P))
        nc.sync.dma_start(out=h0t[:, 4:8, :], in_=h0v[:, 4:8, :])
        cols_bf = []
        for v, vec in enumerate((ln1_g, ln1_b)):
            col_bf = keep.tile([P, NB], BF16, name="col_bf%d" % v)
            with nc.allow_non_contiguous_dma(reason="4 neighbouring channels a piece"):
                nc.sync.dma_start(out=col_bf[:].rearrange("p (g t) -> p g t", t=4), in_=vec.rearrange("(g p t) -> p g t", p=P, t=4))
            cols_bf.append(col_bf)
        z_sb = keep.tile([P, NT, A], BF16, name="z_sb", align_bytes=64)
        k1_sb = keep.tile([P, NT, A], BF16, name="k1_sb", align_bytes=64)
        b2_bc = keep.tile([P, A], BF16, name="b2_bc", align_bytes=64)
        nc.sync.dma_start(out=z_sb[:], in_=z.rearrange("(p i) a -> p i a", i=NT))
        nc.sync.dma_start(out=k1_sb[:], in_=k1.rearrange("(p i) a -> p i a", i=NT))
        nc.sync.dma_start(out=b2_bc[:], in_=b2.partition_broadcast(P))
        w2_raw = keep.tile([P, G, 4, A], BF16, name="w2_raw", align_bytes=64)
        for g in range(G):
            nc.sync.dma_start(out=w2_raw[:, g], in_=W2.rearrange("(g p t) n -> g p t n", p=P, t=4)[g])
        out_v = out.rearrange("(p i) a -> p i a", i=NT)

        tiny_col = keep.tile([P, 1], F32, name="tiny_col")
        nc.gpsimd.tensor_scalar(out=tiny_col[:], in0=neg_half[:], scalar1=-2.0 * TINY, scalar2=0.0, op0=ALU.mult, op1=ALU.add)
        ident_bf = keep.tile([P, P], BF16, name="ident_bf")
        quarter_bf = keep.tile([P, P], BF16, name="quarter_bf")
        ones_bf = keep.tile([P, P], BF16, name="ones_bf")
        nc.gpsimd.tensor_scalar(out=ident_bf[:], in0=ident[:], scalar1=1.0, scalar2=0.0, op0=ALU.mult, op1=ALU.add)
        nc.gpsimd.tensor_scalar(out=quarter_bf[:], in0=ident[:], scalar1=0.25, scalar2=0.0, op0=ALU.mult, op1=ALU.add)
        nc.gpsimd.memset(ones_bf[:], 2.0**-9)
        cols = keep.tile([P, 2, NB], F32, name="cols")
        for v in range(2):
            nc.gpsimd.tensor_scalar(out=cols[:, v, :], in0=cols_bf[v][:], scalar1=1.0, scalar2=0.0, op0=ALU.mult, op1=ALU.add)

        scale_bc = keep.tile([P, U], F32, name="scale_bc", align_bytes=64)
        w_codes = keep.tile([P, 2, G, 512], U32, name="w_codes", align_bytes=64)
        w_scales = keep.tile([P, 2, G, 512], U8, name="w_scales", align_bytes=64)
        w2_codes = keep.tile([P, G, A], U32, name="w2_codes", align_bytes=64)
        w2_scales = keep.tile([P, G, A], U8, name="w2_scales", align_bytes=64)
        base = keep.tile([P, NT, A], F32, name="base", align_bytes=64)
        res = keep.tile([P, NT, A], F32, name="res", align_bytes=64)
        live = {}
        copy_on = {"V": nc.vector.tensor_copy, "S": nc.scalar.copy}

        def t_SB(s):
            bank = psum.tile([P, 4, P], F32, name="sbank", tag="xt", bufs=4)
            for jj in range(4):
                nc.tensor.transpose(bank[:, jj, :], sc_raw[:, 4 * s + jj : 4 * s + jj + 1].to_broadcast([P, P]), ident[:])
            copy_on[who["SB", s]](
                out=scale_bc[:].rearrange("q (p j) -> q p j", j=NB)[:, :, 4 * s : 4 * s + 4],
                in_=bank[:].rearrange("q j p -> q p j"),
            )

        def t_I(c, g, s):
            if (g, s) == (0, 0):
                wg0 = work.tile([P, G, 512, 4], BF16, name="wg", bufs=2, align_bytes=64)
                live["wg", c] = wg0
            wg = live["wg", c][:, g]
            cols_of = slice(256 * s, 256 * (s + 1))
            copy_on[who["I", c, g, s]](
                out=wg[:, cols_of, :].rearrange("p (c i) k -> p c k i", i=4),
                in_=w_raw[c, g][:, :, cols_of].rearrange("p k (c i) -> p c k i", i=4),
            )

        def t_QW(c):
            nc.vector.quantize_mx(
                out=w_codes[:, c].rearrange("p g n -> p (g n)").bitcast(FP8X4),
                scales=w_scales[:, c].rearrange("p g n -> p (g n)"),
                in_=live["wg", c][:].rearrange("p g n k -> p (g n k)"),
            )

        def t_SC(i):
            hs = work.tile([P, U], BF16, name="hs", bufs=4, align_bytes=64)
            nc.vector.tensor_tensor(out=hs[:], in0=h0t[:, i, :].bitcast(FP8), in1=scale_bc[:], op=ALU.mult)
            live["hs", i] = hs

        def t_HT(i):
            if i % 2 == 0:
                hg0 = work.tile([P, 2, G, P, 4], BF16, name="hg", bufs=3, align_bytes=64)
                live["hg", i // 2] = hg0
            hg = live["hg", i // 2][:, i % 2]
            words = live["hs", i][:].bitcast(F32)
            bank = psum.tile([P, G, 2, P], F32, name="hbank", tag="xt", bufs=4)
            for g in range(G):
                for u in range(2):
                    nc.tensor.transpose(bank[:, g, u, :], words[:, 256 * g + u : 256 * (g + 1) : 2], ident[:])
            copy_on[who["HT", i]](out=hg.bitcast(F32), in_=bank[:].rearrange("p g u r -> p g r u"))

        def t_QH(u):
            h_codes = work.tile([P, 2, G, P], U32, name="h_codes", bufs=4, align_bytes=64)
            h_scales = work.tile([P, 2, G, P], U8, name="h_scales", bufs=4, align_bytes=64)
            nc.vector.quantize_mx(
                out=h_codes[:].rearrange("p e g r -> p (e g r)").bitcast(FP8X4),
                scales=h_scales[:].rearrange("p e g r -> p (e g r)"),
                in_=live["hg", u][:].rearrange("p e g r t -> p (e g r t)"),
            )
            live["hq", u] = (h_codes, h_scales)

        def t_B(i, c):
            if c == 0:
                v0 = work.tile([P, 2, 4, P], F32, name="v", bufs=8, align_bytes=64)
                live["v", i] = v0
            v = live["v", i]
            h_codes, h_scales = live["hq", i // 2]
            pre = psum.tile([P, 512], F32, name="pre", tag="pre", bufs=4)
            for g in range(G):
                nc.tensor.matmul_mx(
                    out=pre[:],
                    lhsT=h_codes[:, i % 2, g, :].bitcast(FP8X4),
                    lhsT_scale=h_scales[:, i % 2, g, :],
                    rhs=w_codes[:, c, g, :].bitcast(FP8X4),
                    rhs_scale=w_scales[:, c, g, :],
                    start=(g == 0),
                    stop=(g == G - 1),
                )
            nc.vector.tensor_tensor(
                out=v[:, c], in0=pre[:].rearrange("p (m t) -> p t m", t=4),
                in1=b1_bc[:, 512 * c : 512 * (c + 1)].rearrange("p (m t) -> p t m", t=4), op=ALU.add,
            )

        def t_SG(i, c=None):
            if i // 4 not in live.setdefault("a", {}):
                a0 = work.tile([P, 4, 2, 512], F32, name="a", bufs=2, align_bytes=64)
                live["a"][i // 4] = a0
            a = live["a"][i // 4][:, i % 4]
            half = slice(0, 2) if c is None else slice(c, c + 1)
            nc.scalar.activation(
                out=a[:, half].rearrange("p c n -> p (c n)"),
                in_=live["v", i][:, half].rearrange("p c t m -> p (c t m)"), func=ACT.Sigmoid, scale=-1.0,
            )

        def t_LN(h):
            a = live["a"][h][:].rearrange("p i c n -> p (i c n)")
            nc.scalar.activation(out=a, in_=a, func=ACT.Ln, bias=tiny_col[:, 0:1])

        def t_TH(i):
            a = live["a"][i // 4][:, i % 4].rearrange("p c n -> p (c n)")
            nc.scalar.activation(out=a, in_=a, func=ACT.Tanh, scale=-1.0)

        def t_M(i):
            v, a = live["v", i][:].rearrange("p c t m -> p (c t m)"), live["a"][i // 4][:, i % 4].rearrange("p c n -> p (c n)")
            s1 = work.tile([P, 1], F32, name="s1", bufs=8)
            mean = work.tile([P, 1], F32, name="mean", bufs=8)
            nc.vector.scalar_tensor_tensor(out=v, in0=v, scalar=1.0, in1=a, op0=ALU.mult, op1=ALU.mult, accum_out=s1[:])
            nc.gpsimd.tensor_scalar(out=mean[:], in0=s1[:], scalar1=1.0 / U, scalar2=0.0, op0=ALU.mult, op1=ALU.add)
            live["s1", i] = s1
            live["mean", i] = mean

        def t_SQ(i):
            v, a = live["v", i][:].rearrange("p c t m -> p (c t m)"), live["a"][i // 4][:, i % 4].rearrange("p c n -> p (c n)")
            s2 = work.tile([P, 1], F32, name="s2", bufs=8)
            if who["SQ", i] == "S":
                nc.scalar.activation(out=a, in_=v, func=ACT.Square, scale=-1.0 * U, bias=live["s1", i][:], accum_out=s2[:])
                live["s2", i] = (s2, 1.0 / U**3)
            else:
                nc.vector.scalar_tensor_tensor(out=a, in0=v, scalar=live["mean", i][:], in1=v, op0=ALU.subtract, op1=ALU.mult, accum_out=s2[:])
                live["s2", i] = (s2, 1.0 / U)

        def t_RS(i, on_vector):
            s2, factor = live["s2", i]
            ve = work.tile([P, 1], F32, name="ve", bufs=8)
            rstd = work.tile([P, 1], F32, name="rstd", bufs=8)
            engine = nc.vector if on_vector else nc.gpsimd
            engine.tensor_scalar(out=ve[:], in0=s2[:], scalar1=factor, scalar2=EPS, op0=ALU.mult, op1=ALU.add)
            nc.gpsimd.tensor_tensor(out=rstd[:], in0=ve[:], in1=neg_half[:], op=ALU.pow)
            live["rstd", i] = rstd

        def t_NR(i):
            x = work.tile([P, NB, P], F32, name="x", bufs=5, align_bytes=64)
            nc.vector.tensor_scalar(
                out=x[:].rearrange("p j m -> p (j m)"), in0=live["v", i][:].rearrange("p c t m -> p (c t m)"),
                scalar1=live["mean", i][:], scalar2=live["rstd", i][:], op0=ALU.subtract, op1=ALU.mult,
            )
            live["x", i] = x

        def t_XT(first, n, b):
            per = 4 // n
            if b == 0:
                hp0 = work.tile([P, NB, P * n], BF16, name="hp%d" % n, bufs=3 - n // 2, align_bytes=64)
                live["hp", first] = hp0
            hp = live["hp", first]
            bank = psum.tile([P, per, P * n], F32, name="xbank", tag="xt", bufs=4)
            for jj in range(per):
                for e in range(n):
                    nc.tensor.transpose(bank[:, jj, P * e : P * (e + 1)], live["x", first + e][:, per * b + jj, :], ident[:])
            for jj in range(per):
                j = per * b + jj
                if who["XT", first, b] == "S":
                    nc.scalar.activation(out=hp[:, j, :], in_=bank[:, jj, :], func=ACT.Identity, scale=cols[:, 0, j : j + 1], bias=cols[:, 1, j : j + 1])
                else:
                    nc.vector.tensor_scalar(out=hp[:, j, :], in0=bank[:, jj, :], scalar1=cols[:, 0, j : j + 1], scalar2=cols[:, 1, j : j + 1], op0=ALU.mult, op1=ALU.add)

        def t_IL(first, n, g):
            if g == 0:
                h1g0 = work.tile([P, G, P * n, 4], BF16, name="h1g%d" % n, bufs=3 - n // 2, align_bytes=64)
                live["h1g", first] = h1g0
            nc.vector.tensor_copy(
                out=live["h1g", first][:, g].rearrange("p (c i) t -> p c t i", i=4),
                in_=live["hp", first][:, 4 * g : 4 * g + 4, :].rearrange("p t (c i) -> p c t i", i=4),
            )

        def t_QX(first, n):
            q_codes = work.tile([P, G, P * n], U32, name="q_codes%d" % n, bufs=3 - n // 2, align_bytes=64)
            q_scales = work.tile([P, G, P * n], U8, name="q_scales%d" % n, bufs=3 - n // 2, align_bytes=64)
            nc.vector.quantize_mx(
                out=q_codes[:].rearrange("p g r -> p (g r)").bitcast(FP8X4),
                scales=q_scales[:].rearrange("p g r -> p (g r)"),
                in_=live["h1g", first][:].rearrange("p g r t -> p (g r t)"),
            )
            live["q", first] = (q_codes, q_scales)

        def t_FN(first, n):
            q_codes, q_scales = live["q", first]
            obank = psum.tile([P, n, A], F32, name="obank", tag="xt", bufs=4)
            for e in range(n):
                for g in range(G):
                    nc.tensor.matmul_mx(
                        out=obank[:, e, :],
                        lhsT=q_codes[:, g, P * e : P * (e + 1)].bitcast(FP8X4),
                        lhsT_scale=q_scales[:, g, P * e : P * (e + 1)],
                        rhs=w2_codes[:, g, :].bitcast(FP8X4),
                        rhs_scale=w2_scales[:, g, :],
                        start=(g == 0),
                        stop=(g == G - 1),
                    )
            rows = slice(first, first + n)
            nc.vector.scalar_tensor_tensor(out=res[:, rows, :], in0=obank[:], scalar=0.25, in1=base[:, rows, :], op0=ALU.mult, op1=ALU.add)
            nc.sync.dma_start(out=out_v[:, rows, :], in_=res[:, rows, :])

        def t_WU(n):
            wbank = psum.tile([P, 512], F32, name="wbank", tag="xt", bufs=4)
            for k in range(n):
                nc.tensor.matmul(out=wbank[:], lhsT=ident_bf[:], rhs=w_raw[0, 0][:, k % 4, :], start=(k == 0), stop=(k == n - 1))

        def t_BS(h):
            bank = psum.tile([P, 4, A], F32, name="bbank", tag="xt", bufs=4)
            nc.tensor.matmul(out=bank[:], lhsT=quarter_bf[:], rhs=k1_sb[:, 4 * h : 4 * h + 4, :], start=True, stop=False)
            nc.tensor.matmul(out=bank[:], lhsT=ident_bf[:], rhs=z_sb[:, 4 * h : 4 * h + 4, :], start=False, stop=False)
            nc.tensor.matmul(out=bank[:], lhsT=ones_bf[:], rhs=b2_bc[:].unsqueeze(1).to_broadcast([P, 4, A]), start=False, stop=True)
            copy_on[who["BS", h]](out=base[:, 4 * h : 4 * h + 4, :], in_=bank[:])

        def t_W2(z0):
            w2g = work.tile([P, G, A, 4], BF16, name="w2g", bufs=1, align_bytes=64)
            for g in range(G):
                copy_on[who["W2", 0]](out=w2g[:, g], in_=w2_raw[:, g].rearrange("p k n -> p n k"))
            nc.vector.quantize_mx(
                out=w2_codes[:].rearrange("p g n -> p (g n)").bitcast(FP8X4),
                scales=w2_scales[:].rearrange("p g n -> p (g n)"),
                in_=w2g[:].rearrange("p g n k -> p (g n k)"),
            )

        todo = {"SB": t_SB, "I": t_I, "QW": t_QW, "SC": t_SC, "HT": t_HT, "QH": t_QH, "B": t_B, "SG": t_SG, "LN": t_LN, "TH": t_TH, "M": t_M, "SQ": t_SQ, "NR": t_NR, "RS": t_RS, "XT": t_XT, "IL": t_IL, "QX": t_QX, "FN": t_FN, "BS": t_BS, "WU": t_WU, "W2": t_W2}
        for step in default_order():
            todo[step[0]](*step[1:])
